import numpy as np
import ml_dtypes


def mxq(x, axis, fmt="e4m3"):
    dtype, down = {"e4m3": (ml_dtypes.float8_e4m3fn, 7), "e5m2": (ml_dtypes.float8_e5m2, 14)}[fmt]
    v = np.moveaxis(np.asarray(x, np.float32).astype(ml_dtypes.bfloat16).astype(np.float64), axis, -1)
    blocks = v.reshape(v.shape[:-1] + (-1, 32))
    amax = np.abs(blocks).max(-1, keepdims=True)
    byte = np.maximum(np.where(amax > 0, np.frexp(amax)[1] - 1 + 127, 0) - down, 1)
    scale = np.exp2(byte - 127.0)
    codes = (blocks / scale).astype(np.float32).astype(dtype).astype(np.float64)
    return np.moveaxis((codes * scale).reshape(v.shape), -1, axis)


WIDE = False


def mx_kscale(k):
    if not WIDE:
        return np.ones(k)
    levels = np.array([10, -10, 5, -5, 0])
    a = np.random.permutation(np.resize(levels, k // 512 * 4)).reshape(k // 512, 4)
    idx = np.arange(k)
    return np.exp2(a[idx // 512, idx % 128 // 32])


BF16 = ml_dtypes.bfloat16


def bf(x):
    return np.asarray(x, np.float32).astype(BF16)


def f64(x):
    return np.asarray(x).astype(np.float64)


E2M1 = np.array([0.0, 0.5, 1.0, 1.5, 2.0, 3.0, 4.0, 6.0, -0.0, -0.5, -1.0, -1.5, -2.0, -3.0, -4.0, -6.0])


def pack_weight(w, fmt):
    k, n = w.shape
    w = f64(bf(w)).reshape(k // 32, 32, n)
    amax = np.abs(w).max(1)
    if fmt == "e4m3":
        byte = np.frexp(amax)[1] - 1 + 127 - 7
    else:
        mant, ex = np.frexp(amax / 6.0)
        byte = np.where(mant > 0.5, ex, ex - 1) + 127
    byte = np.clip(np.where(amax > 0, byte, 1), 1, 254)
    scaled = (w * np.exp2(127.0 - byte)[:, None, :]).reshape(k, n).astype(np.float32)
    by_word = np.ascontiguousarray(scaled.reshape(k // 512, 128, 4, n).transpose(0, 1, 3, 2))
    if fmt == "e4m3":
        words = by_word.astype(ml_dtypes.float8_e4m3fn).view(np.uint8)
    else:
        c = by_word.astype(ml_dtypes.float4_e2m1fn).view(np.uint8) & 0xF
        words = c[..., 0::2] | (c[..., 1::2] << 4)
    return np.ascontiguousarray(words), np.ascontiguousarray(byte.astype(np.uint8).reshape(k // 512, 16, n))


def unpack_weight(words, scales, fmt):
    g, p, n, _ = words.shape
    if fmt == "e4m3":
        vals = np.ascontiguousarray(words).view(ml_dtypes.float8_e4m3fn).astype(np.float64)
    else:
        nib = np.empty((g, p, n, 4), np.uint8)
        nib[..., 0::2] = words & 0xF
        nib[..., 1::2] = words >> 4
        vals = E2M1[nib]
    vals = vals * np.repeat(np.exp2(scales.astype(np.float64) - 127.0), 8, axis=1)[..., None]
    return vals.transpose(0, 1, 3, 2).reshape(g * 512, n)


B, D, T, N, H, DH = 2, 512, 1024, 3, 8, 64
EPS = 1e-6
NEG_SLOPE = 0.2


def setup_inputs():
    s = mx_kscale(D)
    x = bf(np.random.standard_normal((B, D, T)) * s[:, None])
    stack = np.random.standard_normal((N, H, D, DH)) * 1.4 / np.sqrt(D) / s[:, None]
    words, scales = pack_weight(stack.reshape(-1, DH), "e4m3")
    norm_w = bf(1.5 + 0.1 * np.random.standard_normal(1))
    return {"x": x, "qkv_words": words, "qkv_scales": scales, "norm_w": norm_w}


def reference(x, qkv_words, qkv_scales, norm_w):
    x = f64(x)
    a = np.where(x >= 0, x, NEG_SLOPE * x)
    aq = mxq(a, 1, "e4m3")
    wq = unpack_weight(qkv_words, qkv_scales, "e4m3").reshape(N, H, D, DH)
    y = aq.transpose(0, 2, 1) @ wq.transpose(2, 0, 1, 3).reshape(D, N * H * DH)
    h = y.reshape(B, T, N, H, DH).transpose(2, 0, 3, 1, 4)
    denom = np.mean(h * h, axis=-2, keepdims=True)
    return f64(norm_w) * (h / np.sqrt(denom + EPS))

@@ -1,0 +1,229 @@
+import concourse.mybir as mybir
+from concourse.masks import make_identity
+
+F32 = mybir.dt.float32
+BF16 = mybir.dt.bfloat16
+I32 = mybir.dt.int32
+U32 = mybir.dt.uint32
+U8 = mybir.dt.uint8
+FP8X4 = mybir.dt.float8_e4m3fn_x4
+ALU = mybir.AluOpType
+ACT = mybir.ActivationFunctionType
+
+B, D, T, N, H, DH = 2, 512, 1024, 3, 8, 64
+EPS = 1e-6
+NEG_SLOPE = 0.2
+FLOPS = 2 * B * T * D * N * H * DH
+
+P = 128
+PACK = 4
+assert D == P * PACK
+M_TILES = T // P
+MATRICES = N * H
+W_COLS = MATRICES * DH
+BANK = 512
+
+GROUP_COLS = 256
+GROUP_HEADS = GROUP_COLS // DH
+GROUP_UNITS = GROUP_COLS // P
+GROUPS_PER_BATCH = W_COLS // GROUP_COLS
+GROUPS = B * GROUPS_PER_BATCH
+T_HALVES = T // BANK
+QUARTERS = GROUP_UNITS * T_HALVES
+TILES_PER_BANK = BANK // GROUP_COLS
+assert QUARTERS * TILES_PER_BANK == M_TILES
+LEAD = 2
+
+
+def tile_mha_pa_e_kernel(tc, x, qkv_words, qkv_scales, norm_w, out):
+    nc = tc.nc
+    with tc.tile_pool(name="keep", bufs=1) as keep, tc.tile_pool(name="small", bufs=4) as small, tc.tile_pool(
+        name="squares", bufs=4
+    ) as squares, tc.tile_pool(name="spread", bufs=3) as spread, tc.tile_pool(name="stage", bufs=3) as stage, tc.psum_pool(
+        name="stat_ps", bufs=3
+    ) as stat_ps, tc.psum_pool(name="spread_ps", bufs=1) as spread_ps, tc.psum_pool(name="out_ps", bufs=4) as out_ps:
+        w_plane = keep.tile([P, W_COLS], U8, align_bytes=64)
+        nc.vector.memset(w_plane[:].bitcast(I32), 0)
+        one = keep.tile([P, 1], F32)
+        nc.vector.memset(one[:], 1.0)
+        warm = keep.tile([P, 1], F32)
+        nc.scalar.activation(out=warm[:], in_=one[:], func=ACT.Sqrt)
+        identity = keep.tile([P, P], F32)
+        make_identity(nc, identity[:])
+        gain_bf16 = keep.tile([P, 1], BF16)
+        nc.scalar.dma_start(out=gain_bf16[:], in_=norm_w.partition_broadcast(P))
+        gain = keep.tile([P, 1], F32)
+        nc.vector.tensor_copy(out=gain[:], in_=gain_bf16[:])
+
+        x_sb = [keep.tile([P, PACK, T], BF16, name="x_sb%d" % b) for b in range(B)]
+        w_words = keep.tile([P, W_COLS], U32, align_bytes=64)
+
+        def load_x(b):
+            rows = x[b].rearrange("(p j) t -> p j t", j=PACK)
+            for half in range(T_HALVES):
+                cols = slice(half * BANK, (half + 1) * BANK)
+                nc.sync.dma_start(out=x_sb[b][:, :, cols], in_=rows[:, :, cols])
+
+        def load_words(n):
+            first = n * H
+            nc.sync.dma_start(
+                out=w_words[:, first * DH : (first + H) * DH].bitcast(I32).rearrange("p (e c) -> p e c", c=DH),
+                in_=qkv_words[first : first + H].rearrange("e p c t -> p e (c t)").bitcast(I32),
+            )
+
+        def load_scales():
+            for quadrant in range(4):
+                nc.sync.dma_start(
+                    out=w_plane[32 * quadrant : 32 * quadrant + 4, :].bitcast(I32).rearrange("r (e c) -> r e c", c=DH // 4),
+                    in_=qkv_scales[:, 4 * quadrant : 4 * quadrant + 4, :].rearrange("e r c -> r e c").bitcast(I32),
+                )
+
+        load_x(0)
+        load_words(0)
+        load_scales()
+        load_x(1)
+        load_words(1)
+        load_words(2)
+
+        a_rows = [keep.tile([P, PACK, T], BF16, name="a_rows%d" % b) for b in range(B)]
+        a_grouped = [keep.tile([P, M_TILES, P, PACK], BF16, name="a_grouped%d" % b, align_bytes=64) for b in range(B)]
+        a_codes = [keep.tile([P, T], U32, name="a_codes%d" % b, align_bytes=64) for b in range(B)]
+        a_plane = [keep.tile([P, T], U8, name="a_plane%d" % b, align_bytes=64) for b in range(B)]
+
+        def leaky_relu(b):
+            for half in range(T_HALVES):
+                cols = slice(half * BANK, (half + 1) * BANK)
+                nc.vector.tensor_scalar_mul(out=a_rows[b][:, :, cols], in0=x_sb[b][:, :, cols], scalar1=NEG_SLOPE)
+                nc.vector.tensor_tensor(out=a_rows[b][:, :, cols], in0=x_sb[b][:, :, cols], in1=a_rows[b][:, :, cols], op=ALU.max)
+
+        def regroup_views(b, half, m_half):
+            q_range = slice(half * (P // 2), (half + 1) * (P // 2))
+            m_range = slice(m_half * (M_TILES // 2), (m_half + 1) * (M_TILES // 2))
+            dst = a_grouped[b][:, m_range, q_range, :].rearrange("p m q j -> p q m j")
+            src = a_rows[b][:].rearrange("p j (q m) -> p q m j", m=M_TILES)[:, q_range, m_range, :]
+            return dst, src
+
+        def quantise(b):
+            for m_half in range(2):
+                m_range = slice(m_half * (M_TILES // 2), (m_half + 1) * (M_TILES // 2))
+                cols = slice(m_half * (T // 2), (m_half + 1) * (T // 2))
+                nc.vector.quantize_mx(
+                    out=a_codes[b][:, cols].bitcast(FP8X4),
+                    scales=a_plane[b][:, cols],
+                    in_=a_grouped[b][:, m_range].rearrange("p m q j -> p (m q j)"),
+                )
+
+        leaky_relu(0)
+        for m_half in range(2):
+            dst, src = regroup_views(0, 0, m_half)
+            nc.scalar.copy(out=dst, in_=src)
+        for m_half in range(2):
+            dst, src = regroup_views(0, 1, m_half)
+            nc.vector.tensor_copy(out=dst, in_=src)
+        quantise(0)
+        leaky_relu(1)
+        for half in range(2):
+            for m_half in range(2):
+                dst, src = regroup_views(1, half, m_half)
+                nc.gpsimd.tensor_scalar(out=dst, in0=src, scalar1=1.0, scalar2=0.0, op0=ALU.mult, op1=ALU.add)
+
+        sums = {}
+        scales = {}
+        staged = {}
+
+        def batch_and_columns(g):
+            return g // GROUPS_PER_BATCH, (g % GROUPS_PER_BATCH) * GROUP_COLS
+
+        def statistics_pass(g, quarter):
+            b, col0 = batch_and_columns(g)
+            unit, half = divmod(quarter, T_HALVES)
+            if quarter == 0:
+                sums[g] = small.tile([P, GROUP_UNITS, T_HALVES], F32, name="sums")
+            w_cols = slice(col0 + unit * P, col0 + (unit + 1) * P)
+            t_cols = slice(half * BANK, (half + 1) * BANK)
+            h_ct = stat_ps.tile([P, BANK], F32, name="h_ct")
+            nc.tensor.matmul_mx(
+                out=h_ct[:],
+                lhsT=w_words[:, w_cols].bitcast(FP8X4),
+                lhsT_scale=w_plane[:, w_cols],
+                rhs=a_codes[b][:, t_cols].bitcast(FP8X4),
+                rhs_scale=a_plane[b][:, t_cols],
+                start=True,
+                stop=True,
+            )
+            unread = squares.tile([P, BANK], BF16, name="unread")
+            nc.scalar.activation(out=unread[:], in_=h_ct[:], func=ACT.Square, accum_out=sums[g][:, unit, half : half + 1])
+
+        def scale_step(g, quarter):
+            if quarter == 0:
+                total = small.tile([P, GROUP_UNITS], F32, name="total")
+                nc.vector.tensor_tensor(out=total[:], in0=sums[g][:, :, 0], in1=sums[g][:, :, 1], op=ALU.add)
+                scales[g] = total
+            elif quarter == 1:
+                rms = small.tile([P, GROUP_UNITS], F32, name="rms")
+                nc.scalar.activation(out=rms[:], in_=scales[g][:], func=ACT.Sqrt, scale=1.0 / T, bias=EPS)
+                scales[g] = rms
+            elif quarter == 2:
+                inverse = small.tile([P, GROUP_UNITS], F32, name="inverse")
+                nc.vector.reciprocal(out=inverse[:], in_=scales[g][:])
+                spread_bank = spread_ps.tile([P, GROUP_COLS], F32, name="spread_bank")
+                for unit in range(GROUP_UNITS):
+                    nc.tensor.matmul(
+                        out=spread_bank[:, unit * P : (unit + 1) * P],
+                        lhsT=inverse[:, unit : unit + 1].to_broadcast([P, P]),
+                        rhs=identity[:],
+                        start=True,
+                        stop=True,
+                    )
+                scales[g] = spread_bank
+            else:
+                scale_row = spread.tile([P, GROUP_COLS], F32, name="scale_row")
+                nc.scalar.activation(out=scale_row[:], in_=scales[g][:], func=ACT.Copy, scale=gain[:, 0:1])
+                scales[g] = scale_row
+
+        def output_bank(g, quarter):
+            b, col0 = batch_and_columns(g)
+            if quarter == 0:
+                staged[g] = stage.tile([P, GROUP_HEADS, M_TILES, DH], F32, name="staged")
+            w_cols = slice(col0, col0 + GROUP_COLS)
+            h_tc = out_ps.tile([P, TILES_PER_BANK, GROUP_COLS], F32, name="h_tc")
+            for i in range(TILES_PER_BANK):
+                m = quarter * TILES_PER_BANK + i
+                t_cols = slice(m * P, (m + 1) * P)
+                nc.tensor.matmul_mx(
+                    out=h_tc[:, i, :],
+                    lhsT=a_codes[b][:, t_cols].bitcast(FP8X4),
+                    lhsT_scale=a_plane[b][:, t_cols],
+                    rhs=w_words[:, w_cols].bitcast(FP8X4),
+                    rhs_scale=w_plane[:, w_cols],
+                    start=True,
+                    stop=True,
+                )
+            m_range = slice(quarter * TILES_PER_BANK, (quarter + 1) * TILES_PER_BANK)
+            nc.vector.tensor_tensor(
+                out=staged[g][:, :, m_range, :].rearrange("p e m j -> p m e j"),
+                in0=h_tc[:].rearrange("p m (e j) -> p m e j", j=DH),
+                in1=scales[g][:].rearrange("p (e j) -> p e j", j=DH).unsqueeze(1).to_broadcast([P, TILES_PER_BANK, GROUP_HEADS, DH]),
+                op=ALU.mult,
+            )
+
+        def store(g):
+            b, col0 = batch_and_columns(g)
+            n, head0 = divmod(col0 // DH, H)
+            nc.sync.dma_start(
+                out=out[n, b, head0 : head0 + GROUP_HEADS].rearrange("e (q m) j -> q e (m j)", m=M_TILES),
+                in_=staged[g][:].rearrange("p e m j -> p e (m j)"),
+            )
+
+        for g in range(-LEAD, GROUPS):
+            if g + LEAD == GROUPS_PER_BATCH:
+                quantise(1)
+            for quarter in range(QUARTERS):
+                if g + LEAD < GROUPS:
+                    statistics_pass(g + LEAD, quarter)
+                if 0 <= g + 1 < GROUPS:
+                    scale_step(g + 1, quarter)
+                if g >= 0:
+                    output_bank(g, quarter)
+            if g >= 0:
+                store(g)

@@ -39,9 +39,9 @@ def tile_mha_pa_e_kernel(tc, x, qkv_words, qkv_scales, norm_w, out):
     nc = tc.nc
     with tc.tile_pool(name="keep", bufs=1) as keep, tc.tile_pool(name="small", bufs=4) as small, tc.tile_pool(
         name="squares", bufs=4
-    ) as squares, tc.tile_pool(name="spread", bufs=3) as spread, tc.tile_pool(name="stage", bufs=3) as stage, tc.psum_pool(
+    ) as squares, tc.tile_pool(name="spread", bufs=3) as spread, tc.tile_pool(name="stage", bufs=4) as stage, tc.psum_pool(
         name="stat_ps", bufs=3
-    ) as stat_ps, tc.psum_pool(name="spread_ps", bufs=1) as spread_ps, tc.psum_pool(name="out_ps", bufs=4) as out_ps:
+    ) as stat_ps, tc.psum_pool(name="spread_ps", bufs=1) as spread_ps, tc.psum_pool(name="out_ps", bufs=4) as out_ps, tc.manual_schedule():
         w_plane = keep.tile([P, W_COLS], U8, align_bytes=64)
         nc.vector.memset(w_plane[:].bitcast(I32), 0)
         one = keep.tile([P, 1], F32)
@@ -154,32 +154,37 @@ def tile_mha_pa_e_kernel(tc, x, qkv_words, qkv_scales, norm_w, out):
             unread = squares.tile([P, BANK], BF16, name="unread")
             nc.scalar.activation(out=unread[:], in_=h_ct[:], func=ACT.Square, accum_out=sums[g][:, unit, half : half + 1])
 
-        def scale_step(g, quarter):
-            if quarter == 0:
-                total = small.tile([P, GROUP_UNITS], F32, name="total")
-                nc.vector.tensor_tensor(out=total[:], in0=sums[g][:, :, 0], in1=sums[g][:, :, 1], op=ALU.add)
-                scales[g] = total
-            elif quarter == 1:
-                rms = small.tile([P, GROUP_UNITS], F32, name="rms")
-                nc.scalar.activation(out=rms[:], in_=scales[g][:], func=ACT.Sqrt, scale=1.0 / T, bias=EPS)
-                scales[g] = rms
-            elif quarter == 2:
-                inverse = small.tile([P, GROUP_UNITS], F32, name="inverse")
-                nc.vector.reciprocal(out=inverse[:], in_=scales[g][:])
-                spread_bank = spread_ps.tile([P, GROUP_COLS], F32, name="spread_bank")
-                for unit in range(GROUP_UNITS):
-                    nc.tensor.matmul(
-                        out=spread_bank[:, unit * P : (unit + 1) * P],
-                        lhsT=inverse[:, unit : unit + 1].to_broadcast([P, P]),
-                        rhs=identity[:],
-                        start=True,
-                        stop=True,
-                    )
-                scales[g] = spread_bank
-            else:
-                scale_row = spread.tile([P, GROUP_COLS], F32, name="scale_row")
-                nc.scalar.activation(out=scale_row[:], in_=scales[g][:], func=ACT.Copy, scale=gain[:, 0:1])
-                scales[g] = scale_row
+        def add_halves(g):
+            total = small.tile([P, GROUP_UNITS], F32, name="total")
+            nc.vector.tensor_tensor(out=total[:], in0=sums[g][:, :, 0], in1=sums[g][:, :, 1], op=ALU.add)
+            scales[g] = total
+
+        def root_of_mean(g):
+            rms = small.tile([P, GROUP_UNITS], F32, name="rms")
+            nc.scalar.activation(out=rms[:], in_=scales[g][:], func=ACT.Sqrt, scale=1.0 / T, bias=EPS)
+            scales[g] = rms
+
+        def invert(g):
+            inverse = small.tile([P, GROUP_UNITS], F32, name="inverse")
+            nc.vector.reciprocal(out=inverse[:], in_=scales[g][:])
+            scales[g] = inverse
+
+        def spread_over_partitions(g):
+            spread_bank = spread_ps.tile([P, GROUP_COLS], F32, name="spread_bank")
+            for unit in range(GROUP_UNITS):
+                nc.tensor.matmul(
+                    out=spread_bank[:, unit * P : (unit + 1) * P],
+                    lhsT=scales[g][:, unit : unit + 1].to_broadcast([P, P]),
+                    rhs=identity[:],
+                    start=True,
+                    stop=True,
+                )
+            scales[g] = spread_bank
+
+        def apply_gain(g):
+            scale_row = spread.tile([P, GROUP_COLS], F32, name="scale_row")
+            nc.vector.tensor_scalar_mul(out=scale_row[:], in0=scales[g][:], scalar1=gain[:, 0:1])
+            scales[g] = scale_row
 
         def output_bank(g, quarter):
             b, col0 = batch_and_columns(g)
@@ -218,12 +223,21 @@ def tile_mha_pa_e_kernel(tc, x, qkv_words, qkv_scales, norm_w, out):
         for g in range(-LEAD, GROUPS):
             if g + LEAD == GROUPS_PER_BATCH:
                 quantise(1)
+            if g >= 0:
+                apply_gain(g)
             for quarter in range(QUARTERS):
+                if 0 <= g + 1 < GROUPS:
+                    if quarter == 0:
+                        add_halves(g + 1)
+                    elif quarter == 1:
+                        root_of_mean(g + 1)
+                    elif quarter == 2:
+                        invert(g + 1)
                 if g + LEAD < GROUPS:
                     statistics_pass(g + LEAD, quarter)
-                if 0 <= g + 1 < GROUPS:
-                    scale_step(g + 1, quarter)
                 if g >= 0:
                     output_bank(g, quarter)
+            if 0 <= g + 1 < GROUPS:
+                spread_over_partitions(g + 1)
             if g >= 0:
                 store(g)

@@ -32,7 +32,10 @@ T_HALVES = T // BANK
 QUARTERS = GROUP_UNITS * T_HALVES
 TILES_PER_BANK = BANK // GROUP_COLS
 assert QUARTERS * TILES_PER_BANK == M_TILES
+assert T_HALVES == 2
 LEAD = 2
+ROOT_OF_1_OVER_T = 1.0 / 32.0
+assert ROOT_OF_1_OVER_T * ROOT_OF_1_OVER_T * T == 1.0
 
 
 def tile_mha_pa_e_kernel(tc, x, qkv_words, qkv_scales, norm_w, out):
@@ -44,16 +47,14 @@ def tile_mha_pa_e_kernel(tc, x, qkv_words, qkv_scales, norm_w, out):
     ) as stat_ps, tc.psum_pool(name="spread_ps", bufs=1) as spread_ps, tc.psum_pool(name="out_ps", bufs=4) as out_ps, tc.manual_schedule():
         w_plane = keep.tile([P, W_COLS], U8, align_bytes=64)
         nc.vector.memset(w_plane[:].bitcast(I32), 0)
+        gain_bf16 = keep.tile([P, 1], BF16)
+        nc.scalar.dma_start(out=gain_bf16[:], in_=norm_w.partition_broadcast(P))
         one = keep.tile([P, 1], F32)
         nc.vector.memset(one[:], 1.0)
         warm = keep.tile([P, 1], F32)
-        nc.scalar.activation(out=warm[:], in_=one[:], func=ACT.Sqrt)
+        nc.scalar.activation(out=warm[:], in_=one[:], func=ACT.Abs_reciprocal_sqrt)
         identity = keep.tile([P, P], F32)
         make_identity(nc, identity[:])
-        gain_bf16 = keep.tile([P, 1], BF16)
-        nc.scalar.dma_start(out=gain_bf16[:], in_=norm_w.partition_broadcast(P))
-        gain = keep.tile([P, 1], F32)
-        nc.vector.tensor_copy(out=gain[:], in_=gain_bf16[:])
 
         x_sb = [keep.tile([P, PACK, T], BF16, name="x_sb%d" % b) for b in range(B)]
         w_words = keep.tile([P, W_COLS], U32, align_bytes=64)
@@ -90,11 +91,10 @@ def tile_mha_pa_e_kernel(tc, x, qkv_words, qkv_scales, norm_w, out):
         a_codes = [keep.tile([P, T], U32, name="a_codes%d" % b, align_bytes=64) for b in range(B)]
         a_plane = [keep.tile([P, T], U8, name="a_plane%d" % b, align_bytes=64) for b in range(B)]
 
-        def leaky_relu(b):
-            for half in range(T_HALVES):
-                cols = slice(half * BANK, (half + 1) * BANK)
-                nc.vector.tensor_scalar_mul(out=a_rows[b][:, :, cols], in0=x_sb[b][:, :, cols], scalar1=NEG_SLOPE)
-                nc.vector.tensor_tensor(out=a_rows[b][:, :, cols], in0=x_sb[b][:, :, cols], in1=a_rows[b][:, :, cols], op=ALU.max)
+        def leaky_relu(b, half):
+            cols = slice(half * BANK, (half + 1) * BANK)
+            nc.vector.tensor_scalar_mul(out=a_rows[b][:, :, cols], in0=x_sb[b][:, :, cols], scalar1=NEG_SLOPE)
+            nc.vector.tensor_tensor(out=a_rows[b][:, :, cols], in0=x_sb[b][:, :, cols], in1=a_rows[b][:, :, cols], op=ALU.max)
 
         def regroup_views(b, half, m_half):
             q_range = slice(half * (P // 2), (half + 1) * (P // 2))
@@ -113,7 +113,8 @@ def tile_mha_pa_e_kernel(tc, x, qkv_words, qkv_scales, norm_w, out):
                     in_=a_grouped[b][:, m_range].rearrange("p m q j -> p (m q j)"),
                 )
 
-        leaky_relu(0)
+        leaky_relu(0, 0)
+        leaky_relu(0, 1)
         for m_half in range(2):
             dst, src = regroup_views(0, 0, m_half)
             nc.scalar.copy(out=dst, in_=src)
@@ -121,8 +122,11 @@ def tile_mha_pa_e_kernel(tc, x, qkv_words, qkv_scales, norm_w, out):
             dst, src = regroup_views(0, 1, m_half)
             nc.vector.tensor_copy(out=dst, in_=src)
         quantise(0)
-        leaky_relu(1)
-        for half in range(2):
+        gain = keep.tile([P, 1], F32)
+        nc.vector.tensor_copy(out=gain[:], in_=gain_bf16[:])
+
+        def prepare_half_of_batch_1(half):
+            leaky_relu(1, half)
             for m_half in range(2):
                 dst, src = regroup_views(1, half, m_half)
                 nc.gpsimd.tensor_scalar(out=dst, in0=src, scalar1=1.0, scalar2=0.0, op0=ALU.mult, op1=ALU.add)
@@ -152,32 +156,27 @@ def tile_mha_pa_e_kernel(tc, x, qkv_words, qkv_scales, norm_w, out):
                 stop=True,
             )
             unread = squares.tile([P, BANK], BF16, name="unread")
-            nc.scalar.activation(out=unread[:], in_=h_ct[:], func=ACT.Square, accum_out=sums[g][:, unit, half : half + 1])
+            nc.scalar.activation(
+                out=unread[:], in_=h_ct[:], func=ACT.Square, scale=ROOT_OF_1_OVER_T, accum_out=sums[g][:, unit, half : half + 1]
+            )
 
         def add_halves(g):
-            total = small.tile([P, GROUP_UNITS], F32, name="total")
-            nc.vector.tensor_tensor(out=total[:], in0=sums[g][:, :, 0], in1=sums[g][:, :, 1], op=ALU.add)
-            scales[g] = total
+            mean = small.tile([P, GROUP_UNITS], F32, name="mean")
+            nc.vector.scalar_tensor_tensor(
+                out=mean[:], in0=sums[g][:, :, 0], scalar=EPS, in1=sums[g][:, :, 1], op0=ALU.add, op1=ALU.add
+            )
+            scales[g] = mean
 
-        def root_of_mean(g):
-            rms = small.tile([P, GROUP_UNITS], F32, name="rms")
-            nc.scalar.activation(out=rms[:], in_=scales[g][:], func=ACT.Sqrt, scale=1.0 / T, bias=EPS)
-            scales[g] = rms
-
-        def invert(g):
+        def inverse_root(g):
             inverse = small.tile([P, GROUP_UNITS], F32, name="inverse")
-            nc.vector.reciprocal(out=inverse[:], in_=scales[g][:])
+            nc.scalar.activation(out=inverse[:], in_=scales[g][:], func=ACT.Abs_reciprocal_sqrt)
             scales[g] = inverse
 
         def spread_over_partitions(g):
             spread_bank = spread_ps.tile([P, GROUP_COLS], F32, name="spread_bank")
             for unit in range(GROUP_UNITS):
-                nc.tensor.matmul(
-                    out=spread_bank[:, unit * P : (unit + 1) * P],
-                    lhsT=scales[g][:, unit : unit + 1].to_broadcast([P, P]),
-                    rhs=identity[:],
-                    start=True,
-                    stop=True,
+                nc.tensor.transpose(
+                    spread_bank[:, unit * P : (unit + 1) * P], scales[g][:, unit : unit + 1].to_broadcast([P, P]), identity[:]
                 )
             scales[g] = spread_bank
 
@@ -229,10 +228,8 @@ def tile_mha_pa_e_kernel(tc, x, qkv_words, qkv_scales, norm_w, out):
                 if 0 <= g + 1 < GROUPS:
                     if quarter == 0:
                         add_halves(g + 1)
-                    elif quarter == 1:
-                        root_of_mean(g + 1)
                     elif quarter == 2:
-                        invert(g + 1)
+                        inverse_root(g + 1)
                 if g + LEAD < GROUPS:
                     statistics_pass(g + LEAD, quarter)
                 if g >= 0:
@@ -241,3 +238,5 @@ def tile_mha_pa_e_kernel(tc, x, qkv_words, qkv_scales, norm_w, out):
                 spread_over_partitions(g + 1)
             if g >= 0:
                 store(g)
+            else:
+                prepare_half_of_batch_1(g + LEAD)

@@ -34,6 +34,10 @@ TILES_PER_BANK = BANK // GROUP_COLS
 assert QUARTERS * TILES_PER_BANK == M_TILES
 assert T_HALVES == 2
 LEAD = 2
+CHUNKS = 4
+CHUNK_T = T // CHUNKS
+CHUNK_Q = P // CHUNKS
+assert CHUNKS % LEAD == 0
 ROOT_OF_1_OVER_T = 1.0 / 32.0
 assert ROOT_OF_1_OVER_T * ROOT_OF_1_OVER_T * T == 1.0
 
@@ -43,26 +47,18 @@ def tile_mha_pa_e_kernel(tc, x, qkv_words, qkv_scales, norm_w, out):
     with tc.tile_pool(name="keep", bufs=1) as keep, tc.tile_pool(name="small", bufs=4) as small, tc.tile_pool(
         name="squares", bufs=4
     ) as squares, tc.tile_pool(name="spread", bufs=3) as spread, tc.tile_pool(name="stage", bufs=4) as stage, tc.psum_pool(
-        name="stat_ps", bufs=3
-    ) as stat_ps, tc.psum_pool(name="spread_ps", bufs=1) as spread_ps, tc.psum_pool(name="out_ps", bufs=4) as out_ps, tc.manual_schedule():
+        name="stat_ps", bufs=4
+    ) as stat_ps, tc.psum_pool(name="out_ps", bufs=4) as out_ps, tc.manual_schedule():
         w_plane = keep.tile([P, W_COLS], U8, align_bytes=64)
         nc.vector.memset(w_plane[:].bitcast(I32), 0)
-        gain_bf16 = keep.tile([P, 1], BF16)
-        nc.scalar.dma_start(out=gain_bf16[:], in_=norm_w.partition_broadcast(P))
-        one = keep.tile([P, 1], F32)
-        nc.vector.memset(one[:], 1.0)
-        warm = keep.tile([P, 1], F32)
-        nc.scalar.activation(out=warm[:], in_=one[:], func=ACT.Abs_reciprocal_sqrt)
-        identity = keep.tile([P, P], F32)
-        make_identity(nc, identity[:])
 
         x_sb = [keep.tile([P, PACK, T], BF16, name="x_sb%d" % b) for b in range(B)]
         w_words = keep.tile([P, W_COLS], U32, align_bytes=64)
 
         def load_x(b):
             rows = x[b].rearrange("(p j) t -> p j t", j=PACK)
-            for half in range(T_HALVES):
-                cols = slice(half * BANK, (half + 1) * BANK)
+            for chunk in range(CHUNKS):
+                cols = slice(chunk * CHUNK_T, (chunk + 1) * CHUNK_T)
                 nc.sync.dma_start(out=x_sb[b][:, :, cols], in_=rows[:, :, cols])
 
         def load_words(n):
@@ -74,30 +70,38 @@ def tile_mha_pa_e_kernel(tc, x, qkv_words, qkv_scales, norm_w, out):
 
         def load_scales():
             for quadrant in range(4):
-                nc.sync.dma_start(
-                    out=w_plane[32 * quadrant : 32 * quadrant + 4, :].bitcast(I32).rearrange("r (e c) -> r e c", c=DH // 4),
-                    in_=qkv_scales[:, 4 * quadrant : 4 * quadrant + 4, :].rearrange("e r c -> r e c").bitcast(I32),
+                nc.scalar.dma_start(
+                    out=w_plane[32 * quadrant : 32 * quadrant + 4, :].bitcast(F32).rearrange("r (e c) -> r e c", c=DH // 4),
+                    in_=qkv_scales[:, 4 * quadrant : 4 * quadrant + 4, :].rearrange("e r c -> r e c").bitcast(F32),
                 )
 
         load_x(0)
-        load_words(0)
         load_scales()
+        load_words(0)
+        gain_bf16 = keep.tile([P, 1], BF16)
+        nc.sync.dma_start(out=gain_bf16[:], in_=norm_w.partition_broadcast(P))
         load_x(1)
         load_words(1)
         load_words(2)
+        identity = keep.tile([P, P], F32)
+        make_identity(nc, identity[:])
+        one = keep.tile([P, 1], F32)
+        nc.vector.memset(one[:], 1.0)
+        warm = keep.tile([P, 1], F32)
+        nc.scalar.activation(out=warm[:], in_=one[:], func=ACT.Abs_reciprocal_sqrt)
 
         a_rows = [keep.tile([P, PACK, T], BF16, name="a_rows%d" % b) for b in range(B)]
         a_grouped = [keep.tile([P, M_TILES, P, PACK], BF16, name="a_grouped%d" % b, align_bytes=64) for b in range(B)]
         a_codes = [keep.tile([P, T], U32, name="a_codes%d" % b, align_bytes=64) for b in range(B)]
         a_plane = [keep.tile([P, T], U8, name="a_plane%d" % b, align_bytes=64) for b in range(B)]
 
-        def leaky_relu(b, half):
-            cols = slice(half * BANK, (half + 1) * BANK)
+        def leaky_relu(b, chunk):
+            cols = slice(chunk * CHUNK_T, (chunk + 1) * CHUNK_T)
             nc.vector.tensor_scalar_mul(out=a_rows[b][:, :, cols], in0=x_sb[b][:, :, cols], scalar1=NEG_SLOPE)
             nc.vector.tensor_tensor(out=a_rows[b][:, :, cols], in0=x_sb[b][:, :, cols], in1=a_rows[b][:, :, cols], op=ALU.max)
 
-        def regroup_views(b, half, m_half):
-            q_range = slice(half * (P // 2), (half + 1) * (P // 2))
+        def regroup_views(b, chunk, m_half):
+            q_range = slice(chunk * CHUNK_Q, (chunk + 1) * CHUNK_Q)
             m_range = slice(m_half * (M_TILES // 2), (m_half + 1) * (M_TILES // 2))
             dst = a_grouped[b][:, m_range, q_range, :].rearrange("p m q j -> p q m j")
             src = a_rows[b][:].rearrange("p j (q m) -> p q m j", m=M_TILES)[:, q_range, m_range, :]
@@ -113,22 +117,23 @@ def tile_mha_pa_e_kernel(tc, x, qkv_words, qkv_scales, norm_w, out):
                     in_=a_grouped[b][:, m_range].rearrange("p m q j -> p (m q j)"),
                 )
 
-        leaky_relu(0, 0)
-        leaky_relu(0, 1)
+        for chunk in range(CHUNKS):
+            leaky_relu(0, chunk)
+        for chunk in range(CHUNKS - 1):
+            for m_half in range(2):
+                dst, src = regroup_views(0, chunk, m_half)
+                nc.scalar.copy(out=dst, in_=src)
         for m_half in range(2):
-            dst, src = regroup_views(0, 0, m_half)
-            nc.scalar.copy(out=dst, in_=src)
-        for m_half in range(2):
-            dst, src = regroup_views(0, 1, m_half)
+            dst, src = regroup_views(0, CHUNKS - 1, m_half)
             nc.vector.tensor_copy(out=dst, in_=src)
         quantise(0)
         gain = keep.tile([P, 1], F32)
         nc.vector.tensor_copy(out=gain[:], in_=gain_bf16[:])
 
-        def prepare_half_of_batch_1(half):
-            leaky_relu(1, half)
+        def prepare_chunk_of_batch_1(chunk):
+            leaky_relu(1, chunk)
             for m_half in range(2):
-                dst, src = regroup_views(1, half, m_half)
+                dst, src = regroup_views(1, chunk, m_half)
                 nc.gpsimd.tensor_scalar(out=dst, in0=src, scalar1=1.0, scalar2=0.0, op0=ALU.mult, op1=ALU.add)
 
         sums = {}
@@ -145,7 +150,7 @@ def tile_mha_pa_e_kernel(tc, x, qkv_words, qkv_scales, norm_w, out):
                 sums[g] = small.tile([P, GROUP_UNITS, T_HALVES], F32, name="sums")
             w_cols = slice(col0 + unit * P, col0 + (unit + 1) * P)
             t_cols = slice(half * BANK, (half + 1) * BANK)
-            h_ct = stat_ps.tile([P, BANK], F32, name="h_ct")
+            h_ct = stat_ps.tile([P, BANK], F32, name="h_ct", tag="h_ct")
             nc.tensor.matmul_mx(
                 out=h_ct[:],
                 lhsT=w_words[:, w_cols].bitcast(FP8X4),
@@ -173,7 +178,7 @@ def tile_mha_pa_e_kernel(tc, x, qkv_words, qkv_scales, norm_w, out):
             scales[g] = inverse
 
         def spread_over_partitions(g):
-            spread_bank = spread_ps.tile([P, GROUP_COLS], F32, name="spread_bank")
+            spread_bank = stat_ps.tile([P, BANK], F32, name="spread_bank", tag="h_ct")
             for unit in range(GROUP_UNITS):
                 nc.tensor.transpose(
                     spread_bank[:, unit * P : (unit + 1) * P], scales[g][:, unit : unit + 1].to_broadcast([P, P]), identity[:]
@@ -182,7 +187,7 @@ def tile_mha_pa_e_kernel(tc, x, qkv_words, qkv_scales, norm_w, out):
 
         def apply_gain(g):
             scale_row = spread.tile([P, GROUP_COLS], F32, name="scale_row")
-            nc.vector.tensor_scalar_mul(out=scale_row[:], in0=scales[g][:], scalar1=gain[:, 0:1])
+            nc.vector.tensor_scalar_mul(out=scale_row[:], in0=scales[g][:, :GROUP_COLS], scalar1=gain[:, 0:1])
             scales[g] = scale_row
 
         def output_bank(g, quarter):
@@ -214,10 +219,11 @@ def tile_mha_pa_e_kernel(tc, x, qkv_words, qkv_scales, norm_w, out):
         def store(g):
             b, col0 = batch_and_columns(g)
             n, head0 = divmod(col0 // DH, H)
-            nc.sync.dma_start(
-                out=out[n, b, head0 : head0 + GROUP_HEADS].rearrange("e (q m) j -> q e (m j)", m=M_TILES),
-                in_=staged[g][:].rearrange("p e m j -> p e (m j)"),
-            )
+            for first in range(0, GROUP_HEADS, 2):
+                nc.sync.dma_start(
+                    out=out[n, b, head0 + first : head0 + first + 2].rearrange("e (q m) j -> q e (m j)", m=M_TILES),
+                    in_=staged[g][:, first : first + 2].rearrange("p e m j -> p e (m j)"),
+                )
 
         for g in range(-LEAD, GROUPS):
             if g + LEAD == GROUPS_PER_BATCH:
@@ -239,4 +245,5 @@ def tile_mha_pa_e_kernel(tc, x, qkv_words, qkv_scales, norm_w, out):
             if g >= 0:
                 store(g)
             else:
-                prepare_half_of_batch_1(g + LEAD)
+                for chunk in range((g + LEAD) * CHUNKS // LEAD, (g + LEAD + 1) * CHUNKS // LEAD):
+                    prepare_chunk_of_batch_1(chunk)

@@ -34,10 +34,6 @@ TILES_PER_BANK = BANK // GROUP_COLS
 assert QUARTERS * TILES_PER_BANK == M_TILES
 assert T_HALVES == 2
 LEAD = 2
-CHUNKS = 4
-CHUNK_T = T // CHUNKS
-CHUNK_Q = P // CHUNKS
-assert CHUNKS % LEAD == 0
 ROOT_OF_1_OVER_T = 1.0 / 32.0
 assert ROOT_OF_1_OVER_T * ROOT_OF_1_OVER_T * T == 1.0
 
@@ -47,18 +43,26 @@ def tile_mha_pa_e_kernel(tc, x, qkv_words, qkv_scales, norm_w, out):
     with tc.tile_pool(name="keep", bufs=1) as keep, tc.tile_pool(name="small", bufs=4) as small, tc.tile_pool(
         name="squares", bufs=4
     ) as squares, tc.tile_pool(name="spread", bufs=3) as spread, tc.tile_pool(name="stage", bufs=4) as stage, tc.psum_pool(
-        name="stat_ps", bufs=4
-    ) as stat_ps, tc.psum_pool(name="out_ps", bufs=4) as out_ps, tc.manual_schedule():
+        name="stat_ps", bufs=3
+    ) as stat_ps, tc.psum_pool(name="spread_ps", bufs=1) as spread_ps, tc.psum_pool(name="out_ps", bufs=4) as out_ps, tc.manual_schedule():
         w_plane = keep.tile([P, W_COLS], U8, align_bytes=64)
         nc.vector.memset(w_plane[:].bitcast(I32), 0)
+        gain_bf16 = keep.tile([P, 1], BF16)
+        nc.scalar.dma_start(out=gain_bf16[:], in_=norm_w.partition_broadcast(P))
+        one = keep.tile([P, 1], F32)
+        nc.vector.memset(one[:], 1.0)
+        warm = keep.tile([P, 1], F32)
+        nc.scalar.activation(out=warm[:], in_=one[:], func=ACT.Abs_reciprocal_sqrt)
+        identity = keep.tile([P, P], F32)
+        make_identity(nc, identity[:])
 
         x_sb = [keep.tile([P, PACK, T], BF16, name="x_sb%d" % b) for b in range(B)]
         w_words = keep.tile([P, W_COLS], U32, align_bytes=64)
 
         def load_x(b):
             rows = x[b].rearrange("(p j) t -> p j t", j=PACK)
-            for chunk in range(CHUNKS):
-                cols = slice(chunk * CHUNK_T, (chunk + 1) * CHUNK_T)
+            for half in range(T_HALVES):
+                cols = slice(half * BANK, (half + 1) * BANK)
                 nc.sync.dma_start(out=x_sb[b][:, :, cols], in_=rows[:, :, cols])
 
         def load_words(n):
@@ -70,38 +74,30 @@ def tile_mha_pa_e_kernel(tc, x, qkv_words, qkv_scales, norm_w, out):
 
         def load_scales():
             for quadrant in range(4):
-                nc.scalar.dma_start(
-                    out=w_plane[32 * quadrant : 32 * quadrant + 4, :].bitcast(F32).rearrange("r (e c) -> r e c", c=DH // 4),
-                    in_=qkv_scales[:, 4 * quadrant : 4 * quadrant + 4, :].rearrange("e r c -> r e c").bitcast(F32),
+                nc.sync.dma_start(
+                    out=w_plane[32 * quadrant : 32 * quadrant + 4, :].bitcast(I32).rearrange("r (e c) -> r e c", c=DH // 4),
+                    in_=qkv_scales[:, 4 * quadrant : 4 * quadrant + 4, :].rearrange("e r c -> r e c").bitcast(I32),
                 )
 
         load_x(0)
-        load_scales()
         load_words(0)
-        gain_bf16 = keep.tile([P, 1], BF16)
-        nc.sync.dma_start(out=gain_bf16[:], in_=norm_w.partition_broadcast(P))
+        load_scales()
         load_x(1)
         load_words(1)
         load_words(2)
-        identity = keep.tile([P, P], F32)
-        make_identity(nc, identity[:])
-        one = keep.tile([P, 1], F32)
-        nc.vector.memset(one[:], 1.0)
-        warm = keep.tile([P, 1], F32)
-        nc.scalar.activation(out=warm[:], in_=one[:], func=ACT.Abs_reciprocal_sqrt)
 
         a_rows = [keep.tile([P, PACK, T], BF16, name="a_rows%d" % b) for b in range(B)]
         a_grouped = [keep.tile([P, M_TILES, P, PACK], BF16, name="a_grouped%d" % b, align_bytes=64) for b in range(B)]
         a_codes = [keep.tile([P, T], U32, name="a_codes%d" % b, align_bytes=64) for b in range(B)]
         a_plane = [keep.tile([P, T], U8, name="a_plane%d" % b, align_bytes=64) for b in range(B)]
 
-        def leaky_relu(b, chunk):
-            cols = slice(chunk * CHUNK_T, (chunk + 1) * CHUNK_T)
+        def leaky_relu(b, half):
+            cols = slice(half * BANK, (half + 1) * BANK)
             nc.vector.tensor_scalar_mul(out=a_rows[b][:, :, cols], in0=x_sb[b][:, :, cols], scalar1=NEG_SLOPE)
             nc.vector.tensor_tensor(out=a_rows[b][:, :, cols], in0=x_sb[b][:, :, cols], in1=a_rows[b][:, :, cols], op=ALU.max)
 
-        def regroup_views(b, chunk, m_half):
-            q_range = slice(chunk * CHUNK_Q, (chunk + 1) * CHUNK_Q)
+        def regroup_views(b, half, m_half):
+            q_range = slice(half * (P // 2), (half + 1) * (P // 2))
             m_range = slice(m_half * (M_TILES // 2), (m_half + 1) * (M_TILES // 2))
             dst = a_grouped[b][:, m_range, q_range, :].rearrange("p m q j -> p q m j")
             src = a_rows[b][:].rearrange("p j (q m) -> p q m j", m=M_TILES)[:, q_range, m_range, :]
@@ -117,23 +113,22 @@ def tile_mha_pa_e_kernel(tc, x, qkv_words, qkv_scales, norm_w, out):
                     in_=a_grouped[b][:, m_range].rearrange("p m q j -> p (m q j)"),
                 )
 
-        for chunk in range(CHUNKS):
-            leaky_relu(0, chunk)
-        for chunk in range(CHUNKS - 1):
-            for m_half in range(2):
-                dst, src = regroup_views(0, chunk, m_half)
-                nc.scalar.copy(out=dst, in_=src)
+        leaky_relu(0, 0)
+        leaky_relu(0, 1)
         for m_half in range(2):
-            dst, src = regroup_views(0, CHUNKS - 1, m_half)
+            dst, src = regroup_views(0, 0, m_half)
+            nc.scalar.copy(out=dst, in_=src)
+        for m_half in range(2):
+            dst, src = regroup_views(0, 1, m_half)
             nc.vector.tensor_copy(out=dst, in_=src)
         quantise(0)
         gain = keep.tile([P, 1], F32)
         nc.vector.tensor_copy(out=gain[:], in_=gain_bf16[:])
 
-        def prepare_chunk_of_batch_1(chunk):
-            leaky_relu(1, chunk)
+        def prepare_half_of_batch_1(half):
+            leaky_relu(1, half)
             for m_half in range(2):
-                dst, src = regroup_views(1, chunk, m_half)
+                dst, src = regroup_views(1, half, m_half)
                 nc.gpsimd.tensor_scalar(out=dst, in0=src, scalar1=1.0, scalar2=0.0, op0=ALU.mult, op1=ALU.add)
 
         sums = {}
@@ -150,7 +145,7 @@ def tile_mha_pa_e_kernel(tc, x, qkv_words, qkv_scales, norm_w, out):
                 sums[g] = small.tile([P, GROUP_UNITS, T_HALVES], F32, name="sums")
             w_cols = slice(col0 + unit * P, col0 + (unit + 1) * P)
             t_cols = slice(half * BANK, (half + 1) * BANK)
-            h_ct = stat_ps.tile([P, BANK], F32, name="h_ct", tag="h_ct")
+            h_ct = stat_ps.tile([P, BANK], F32, name="h_ct")
             nc.tensor.matmul_mx(
                 out=h_ct[:],
                 lhsT=w_words[:, w_cols].bitcast(FP8X4),
@@ -178,7 +173,7 @@ def tile_mha_pa_e_kernel(tc, x, qkv_words, qkv_scales, norm_w, out):
             scales[g] = inverse
 
         def spread_over_partitions(g):
-            spread_bank = stat_ps.tile([P, BANK], F32, name="spread_bank", tag="h_ct")
+            spread_bank = spread_ps.tile([P, GROUP_COLS], F32, name="spread_bank")
             for unit in range(GROUP_UNITS):
                 nc.tensor.transpose(
                     spread_bank[:, unit * P : (unit + 1) * P], scales[g][:, unit : unit + 1].to_broadcast([P, P]), identity[:]
@@ -187,7 +182,7 @@ def tile_mha_pa_e_kernel(tc, x, qkv_words, qkv_scales, norm_w, out):
 
         def apply_gain(g):
             scale_row = spread.tile([P, GROUP_COLS], F32, name="scale_row")
-            nc.vector.tensor_scalar_mul(out=scale_row[:], in0=scales[g][:, :GROUP_COLS], scalar1=gain[:, 0:1])
+            nc.scalar.activation(out=scale_row[:], in_=scales[g][:], func=ACT.Copy, scale=gain[:, 0:1])
             scales[g] = scale_row
 
         def output_bank(g, quarter):
@@ -219,11 +214,10 @@ def tile_mha_pa_e_kernel(tc, x, qkv_words, qkv_scales, norm_w, out):
         def store(g):
             b, col0 = batch_and_columns(g)
             n, head0 = divmod(col0 // DH, H)
-            for first in range(0, GROUP_HEADS, 2):
-                nc.sync.dma_start(
-                    out=out[n, b, head0 + first : head0 + first + 2].rearrange("e (q m) j -> q e (m j)", m=M_TILES),
-                    in_=staged[g][:, first : first + 2].rearrange("p e m j -> p e (m j)"),
-                )
+            nc.sync.dma_start(
+                out=out[n, b, head0 : head0 + GROUP_HEADS].rearrange("e (q m) j -> q e (m j)", m=M_TILES),
+                in_=staged[g][:].rearrange("p e m j -> p e (m j)"),
+            )
 
         for g in range(-LEAD, GROUPS):
             if g + LEAD == GROUPS_PER_BATCH:
@@ -245,5 +239,4 @@ def tile_mha_pa_e_kernel(tc, x, qkv_words, qkv_scales, norm_w, out):
             if g >= 0:
                 store(g)
             else:
-                for chunk in range((g + LEAD) * CHUNKS // LEAD, (g + LEAD + 1) * CHUNKS // LEAD):
-                    prepare_chunk_of_batch_1(chunk)
+                prepare_half_of_batch_1(g + LEAD)

@@ -44,7 +44,7 @@ def tile_mha_pa_e_kernel(tc, x, qkv_words, qkv_scales, norm_w, out):
         name="squares", bufs=4
     ) as squares, tc.tile_pool(name="spread", bufs=3) as spread, tc.tile_pool(name="stage", bufs=4) as stage, tc.psum_pool(
         name="stat_ps", bufs=3
-    ) as stat_ps, tc.psum_pool(name="spread_ps", bufs=1) as spread_ps, tc.psum_pool(name="out_ps", bufs=4) as out_ps, tc.manual_schedule():
+    ) as stat_ps, tc.psum_pool(name="spread_ps", bufs=1) as spread_ps, tc.psum_pool(name="out_ps", bufs=4) as out_ps:
         w_plane = keep.tile([P, W_COLS], U8, align_bytes=64)
         nc.vector.memset(w_plane[:].bitcast(I32), 0)
         gain_bf16 = keep.tile([P, 1], BF16)

@@ -48,7 +48,6 @@ def tile_mha_pa_e_kernel(tc, x, qkv_words, qkv_scales, norm_w, out):
         w_plane = keep.tile([P, W_COLS], U8, align_bytes=64)
         nc.vector.memset(w_plane[:].bitcast(I32), 0)
         gain_bf16 = keep.tile([P, 1], BF16)
-        nc.scalar.dma_start(out=gain_bf16[:], in_=norm_w.partition_broadcast(P))
         one = keep.tile([P, 1], F32)
         nc.vector.memset(one[:], 1.0)
         warm = keep.tile([P, 1], F32)
@@ -82,6 +81,7 @@ def tile_mha_pa_e_kernel(tc, x, qkv_words, qkv_scales, norm_w, out):
         load_x(0)
         load_words(0)
         load_scales()
+        nc.sync.dma_start(out=gain_bf16[:], in_=norm_w.partition_broadcast(P))
         load_x(1)
         load_words(1)
         load_words(2)
@@ -123,7 +123,7 @@ def tile_mha_pa_e_kernel(tc, x, qkv_words, qkv_scales, norm_w, out):
             nc.vector.tensor_copy(out=dst, in_=src)
         quantise(0)
         gain = keep.tile([P, 1], F32)
-        nc.vector.tensor_copy(out=gain[:], in_=gain_bf16[:])
+        nc.gpsimd.tensor_copy(out=gain[:], in_=gain_bf16[:])
 
         def prepare_half_of_batch_1(half):
             leaky_relu(1, half)

@@ -50,6 +50,8 @@ def tile_mha_pa_e_kernel(tc, x, qkv_words, qkv_scales, norm_w, out):
         gain_bf16 = keep.tile([P, 1], BF16)
         one = keep.tile([P, 1], F32)
         nc.vector.memset(one[:], 1.0)
+        eps = keep.tile([P, 1], F32)
+        nc.vector.memset(eps[:], EPS)
         warm = keep.tile([P, 1], F32)
         nc.scalar.activation(out=warm[:], in_=one[:], func=ACT.Abs_reciprocal_sqrt)
         identity = keep.tile([P, P], F32)
@@ -125,11 +127,11 @@ def tile_mha_pa_e_kernel(tc, x, qkv_words, qkv_scales, norm_w, out):
         gain = keep.tile([P, 1], F32)
         nc.gpsimd.tensor_copy(out=gain[:], in_=gain_bf16[:])
 
-        def prepare_half_of_batch_1(half):
-            leaky_relu(1, half)
-            for m_half in range(2):
-                dst, src = regroup_views(1, half, m_half)
-                nc.gpsimd.tensor_scalar(out=dst, in0=src, scalar1=1.0, scalar2=0.0, op0=ALU.mult, op1=ALU.add)
+        def regroup_batch_1():
+            for half in range(T_HALVES):
+                for m_half in range(2):
+                    dst, src = regroup_views(1, half, m_half)
+                    nc.gpsimd.tensor_scalar(out=dst, in0=src, scalar1=1.0, scalar2=0.0, op0=ALU.mult, op1=ALU.add)
 
         sums = {}
         scales = {}
@@ -162,14 +164,12 @@ def tile_mha_pa_e_kernel(tc, x, qkv_words, qkv_scales, norm_w, out):
 
         def add_halves(g):
             mean = small.tile([P, GROUP_UNITS], F32, name="mean")
-            nc.vector.scalar_tensor_tensor(
-                out=mean[:], in0=sums[g][:, :, 0], scalar=EPS, in1=sums[g][:, :, 1], op0=ALU.add, op1=ALU.add
-            )
+            nc.vector.tensor_reduce(out=mean[:], in_=sums[g][:], op=ALU.add, axis=mybir.AxisListType.X)
             scales[g] = mean
 
         def inverse_root(g):
             inverse = small.tile([P, GROUP_UNITS], F32, name="inverse")
-            nc.scalar.activation(out=inverse[:], in_=scales[g][:], func=ACT.Abs_reciprocal_sqrt)
+            nc.scalar.activation(out=inverse[:], in_=scales[g][:], func=ACT.Abs_reciprocal_sqrt, bias=eps[:, 0:1])
             scales[g] = inverse
 
         def spread_over_partitions(g):
@@ -239,4 +239,6 @@ def tile_mha_pa_e_kernel(tc, x, qkv_words, qkv_scales, norm_w, out):
             if g >= 0:
                 store(g)
             else:
-                prepare_half_of_batch_1(g + LEAD)
+                leaky_relu(1, g + LEAD)
+                if g == -1:
+                    regroup_batch_1()

@@ -33,6 +33,7 @@ QUARTERS = GROUP_UNITS * T_HALVES
 TILES_PER_BANK = BANK // GROUP_COLS
 assert QUARTERS * TILES_PER_BANK == M_TILES
 assert T_HALVES == 2
+FIRST_SUM_ON_GPSIMD = 4
 LEAD = 2
 ROOT_OF_1_OVER_T = 1.0 / 32.0
 assert ROOT_OF_1_OVER_T * ROOT_OF_1_OVER_T * T == 1.0
@@ -164,7 +165,10 @@ def tile_mha_pa_e_kernel(tc, x, qkv_words, qkv_scales, norm_w, out):
 
         def add_halves(g):
             mean = small.tile([P, GROUP_UNITS], F32, name="mean")
-            nc.vector.tensor_reduce(out=mean[:], in_=sums[g][:], op=ALU.add, axis=mybir.AxisListType.X)
+            if g < FIRST_SUM_ON_GPSIMD:
+                nc.vector.tensor_reduce(out=mean[:], in_=sums[g][:], op=ALU.add, axis=mybir.AxisListType.X)
+            else:
+                nc.gpsimd.tensor_tensor(out=mean[:], in0=sums[g][:, :, 0], in1=sums[g][:, :, 1], op=ALU.add)
             scales[g] = mean
 
         def inverse_root(g):

@@ -208,12 +208,15 @@ def tile_mha_pa_e_kernel(tc, x, qkv_words, qkv_scales, norm_w, out):
                     stop=True,
                 )
             m_range = slice(quarter * TILES_PER_BANK, (quarter + 1) * TILES_PER_BANK)
-            nc.vector.tensor_tensor(
-                out=staged[g][:, :, m_range, :].rearrange("p e m j -> p m e j"),
-                in0=h_tc[:].rearrange("p m (e j) -> p m e j", j=DH),
-                in1=scales[g][:].rearrange("p (e j) -> p e j", j=DH).unsqueeze(1).to_broadcast([P, TILES_PER_BANK, GROUP_HEADS, DH]),
-                op=ALU.mult,
+            target = staged[g][:, :, m_range, :].rearrange("p e m j -> p m e j")
+            scale_rows = (
+                scales[g][:].rearrange("p (e j) -> p e j", j=DH).unsqueeze(1).to_broadcast([P, TILES_PER_BANK, GROUP_HEADS, DH])
             )
+            if g + LEAD >= GROUPS and quarter == 0:
+                nc.scalar.copy(out=target, in_=h_tc[:].rearrange("p m (e j) -> p m e j", j=DH))
+                nc.gpsimd.tensor_tensor(out=target, in0=target, in1=scale_rows, op=ALU.mult)
+                return
+            nc.vector.tensor_tensor(out=target, in0=h_tc[:].rearrange("p m (e j) -> p m e j", j=DH), in1=scale_rows, op=ALU.mult)
 
         def store(g):
             b, col0 = batch_and_columns(g)

import concourse.mybir as mybir
from concourse.masks import make_identity

F32 = mybir.dt.float32
BF16 = mybir.dt.bfloat16
I32 = mybir.dt.int32
U32 = mybir.dt.uint32
U8 = mybir.dt.uint8
FP8X4 = mybir.dt.float8_e4m3fn_x4
ALU = mybir.AluOpType
ACT = mybir.ActivationFunctionType

B, D, T, N, H, DH = 2, 512, 1024, 3, 8, 64
EPS = 1e-6
NEG_SLOPE = 0.2
FLOPS = 2 * B * T * D * N * H * DH

P = 128
PACK = 4
assert D == P * PACK
M_TILES = T // P
MATRICES = N * H
W_COLS = MATRICES * DH
BANK = 512

GROUP_COLS = 256
GROUP_HEADS = GROUP_COLS // DH
GROUP_UNITS = GROUP_COLS // P
GROUPS_PER_BATCH = W_COLS // GROUP_COLS
GROUPS = B * GROUPS_PER_BATCH
T_HALVES = T // BANK
QUARTERS = GROUP_UNITS * T_HALVES
TILES_PER_BANK = BANK // GROUP_COLS
assert QUARTERS * TILES_PER_BANK == M_TILES
assert T_HALVES == 2
FIRST_SUM_ON_GPSIMD = 4
LEAD = 2
ROOT_OF_1_OVER_T = 1.0 / 32.0
assert ROOT_OF_1_OVER_T * ROOT_OF_1_OVER_T * T == 1.0


def tile_mha_pa_e_kernel(tc, x, qkv_words, qkv_scales, norm_w, out):
    nc = tc.nc
    with tc.tile_pool(name="keep", bufs=1) as keep, tc.tile_pool(name="small", bufs=4) as small, tc.tile_pool(
        name="squares", bufs=4
    ) as squares, tc.tile_pool(name="spread", bufs=3) as spread, tc.tile_pool(name="stage", bufs=4) as stage, tc.psum_pool(
        name="stat_ps", bufs=3
    ) as stat_ps, tc.psum_pool(name="spread_ps", bufs=1) as spread_ps, tc.psum_pool(name="out_ps", bufs=4) as out_ps:
        w_plane = keep.tile([P, W_COLS], U8, align_bytes=64)
        nc.vector.memset(w_plane[:].bitcast(I32), 0)
        gain_bf16 = keep.tile([P, 1], BF16)
        one = keep.tile([P, 1], F32)
        nc.vector.memset(one[:], 1.0)
        eps = keep.tile([P, 1], F32)
        nc.vector.memset(eps[:], EPS)
        warm = keep.tile([P, 1], F32)
        nc.scalar.activation(out=warm[:], in_=one[:], func=ACT.Abs_reciprocal_sqrt)
        identity = keep.tile([P, P], F32)
        make_identity(nc, identity[:])

        x_sb = [keep.tile([P, PACK, T], BF16, name="x_sb%d" % b) for b in range(B)]
        w_words = keep.tile([P, W_COLS], U32, align_bytes=64)

        def load_x(b):
            rows = x[b].rearrange("(p j) t -> p j t", j=PACK)
            for half in range(T_HALVES):
                cols = slice(half * BANK, (half + 1) * BANK)
                nc.sync.dma_start(out=x_sb[b][:, :, cols], in_=rows[:, :, cols])

        def load_words(n):
            first = n * H
            nc.sync.dma_start(
                out=w_words[:, first * DH : (first + H) * DH].bitcast(I32).rearrange("p (e c) -> p e c", c=DH),
                in_=qkv_words[first : first + H].rearrange("e p c t -> p e (c t)").bitcast(I32),
            )

        def load_scales():
            for quadrant in range(4):
                nc.sync.dma_start(
                    out=w_plane[32 * quadrant : 32 * quadrant + 4, :].bitcast(I32).rearrange("r (e c) -> r e c", c=DH // 4),
                    in_=qkv_scales[:, 4 * quadrant : 4 * quadrant + 4, :].rearrange("e r c -> r e c").bitcast(I32),
                )

        load_x(0)
        load_words(0)
        load_scales()
        nc.sync.dma_start(out=gain_bf16[:], in_=norm_w.partition_broadcast(P))
        load_x(1)
        load_words(1)
        load_words(2)

        a_rows = [keep.tile([P, PACK, T], BF16, name="a_rows%d" % b) for b in range(B)]
        a_grouped = [keep.tile([P, M_TILES, P, PACK], BF16, name="a_grouped%d" % b, align_bytes=64) for b in range(B)]
        a_codes = [keep.tile([P, T], U32, name="a_codes%d" % b, align_bytes=64) for b in range(B)]
        a_plane = [keep.tile([P, T], U8, name="a_plane%d" % b, align_bytes=64) for b in range(B)]

        def leaky_relu(b, half):
            cols = slice(half * BANK, (half + 1) * BANK)
            nc.vector.tensor_scalar_mul(out=a_rows[b][:, :, cols], in0=x_sb[b][:, :, cols], scalar1=NEG_SLOPE)
            nc.vector.tensor_tensor(out=a_rows[b][:, :, cols], in0=x_sb[b][:, :, cols], in1=a_rows[b][:, :, cols], op=ALU.max)

        def regroup_views(b, half, m_half):
            q_range = slice(half * (P // 2), (half + 1) * (P // 2))
            m_range = slice(m_half * (M_TILES // 2), (m_half + 1) * (M_TILES // 2))
            dst = a_grouped[b][:, m_range, q_range, :].rearrange("p m q j -> p q m j")
            src = a_rows[b][:].rearrange("p j (q m) -> p q m j", m=M_TILES)[:, q_range, m_range, :]
            return dst, src

        def quantise(b):
            for m_half in range(2):
                m_range = slice(m_half * (M_TILES // 2), (m_half + 1) * (M_TILES // 2))
                cols = slice(m_half * (T // 2), (m_half + 1) * (T // 2))
                nc.vector.quantize_mx(
                    out=a_codes[b][:, cols].bitcast(FP8X4),
                    scales=a_plane[b][:, cols],
                    in_=a_grouped[b][:, m_range].rearrange("p m q j -> p (m q j)"),
                )

        leaky_relu(0, 0)
        leaky_relu(0, 1)
        for m_half in range(2):
            dst, src = regroup_views(0, 0, m_half)
            nc.scalar.copy(out=dst, in_=src)
        for m_half in range(2):
            dst, src = regroup_views(0, 1, m_half)
            nc.vector.tensor_copy(out=dst, in_=src)
        quantise(0)
        gain = keep.tile([P, 1], F32)
        nc.gpsimd.tensor_copy(out=gain[:], in_=gain_bf16[:])

        def regroup_batch_1():
            for half in range(T_HALVES):
                for m_half in range(2):
                    dst, src = regroup_views(1, half, m_half)
                    nc.gpsimd.tensor_scalar(out=dst, in0=src, scalar1=1.0, scalar2=0.0, op0=ALU.mult, op1=ALU.add)

        sums = {}
        scales = {}
        staged = {}

        def batch_and_columns(g):
            return g // GROUPS_PER_BATCH, (g % GROUPS_PER_BATCH) * GROUP_COLS

        def statistics_pass(g, quarter):
            b, col0 = batch_and_columns(g)
            unit, half = divmod(quarter, T_HALVES)
            if quarter == 0:
                sums[g] = small.tile([P, GROUP_UNITS, T_HALVES], F32, name="sums")
            w_cols = slice(col0 + unit * P, col0 + (unit + 1) * P)
            t_cols = slice(half * BANK, (half + 1) * BANK)
            h_ct = stat_ps.tile([P, BANK], F32, name="h_ct")
            nc.tensor.matmul_mx(
                out=h_ct[:],
                lhsT=w_words[:, w_cols].bitcast(FP8X4),
                lhsT_scale=w_plane[:, w_cols],
                rhs=a_codes[b][:, t_cols].bitcast(FP8X4),
                rhs_scale=a_plane[b][:, t_cols],
                start=True,
                stop=True,
            )
            unread = squares.tile([P, BANK], BF16, name="unread")
            nc.scalar.activation(
                out=unread[:], in_=h_ct[:], func=ACT.Square, scale=ROOT_OF_1_OVER_T, accum_out=sums[g][:, unit, half : half + 1]
            )

        def add_halves(g):
            mean = small.tile([P, GROUP_UNITS], F32, name="mean")
            if g < FIRST_SUM_ON_GPSIMD:
                nc.vector.tensor_reduce(out=mean[:], in_=sums[g][:], op=ALU.add, axis=mybir.AxisListType.X)
            else:
                nc.gpsimd.tensor_tensor(out=mean[:], in0=sums[g][:, :, 0], in1=sums[g][:, :, 1], op=ALU.add)
            scales[g] = mean

        def inverse_root(g):
            inverse = small.tile([P, GROUP_UNITS], F32, name="inverse")
            nc.scalar.activation(out=inverse[:], in_=scales[g][:], func=ACT.Abs_reciprocal_sqrt, bias=eps[:, 0:1])
            scales[g] = inverse

        def spread_over_partitions(g):
            spread_bank = spread_ps.tile([P, GROUP_COLS], F32, name="spread_bank")
            for unit in range(GROUP_UNITS):
                nc.tensor.transpose(
                    spread_bank[:, unit * P : (unit + 1) * P], scales[g][:, unit : unit + 1].to_broadcast([P, P]), identity[:]
                )
            scales[g] = spread_bank

        def apply_gain(g):
            scale_row = spread.tile([P, GROUP_COLS], F32, name="scale_row")
            nc.scalar.activation(out=scale_row[:], in_=scales[g][:], func=ACT.Copy, scale=gain[:, 0:1])
            scales[g] = scale_row

        def output_bank(g, quarter):
            b, col0 = batch_and_columns(g)
            if quarter == 0:
                staged[g] = stage.tile([P, GROUP_HEADS, M_TILES, DH], F32, name="staged")
            w_cols = slice(col0, col0 + GROUP_COLS)
            h_tc = out_ps.tile([P, TILES_PER_BANK, GROUP_COLS], F32, name="h_tc")
            for i in range(TILES_PER_BANK):
                m = quarter * TILES_PER_BANK + i
                t_cols = slice(m * P, (m + 1) * P)
                nc.tensor.matmul_mx(
                    out=h_tc[:, i, :],
                    lhsT=a_codes[b][:, t_cols].bitcast(FP8X4),
                    lhsT_scale=a_plane[b][:, t_cols],
                    rhs=w_words[:, w_cols].bitcast(FP8X4),
                    rhs_scale=w_plane[:, w_cols],
                    start=True,
                    stop=True,
                )
            m_range = slice(quarter * TILES_PER_BANK, (quarter + 1) * TILES_PER_BANK)
            target = staged[g][:, :, m_range, :].rearrange("p e m j -> p m e j")
            scale_rows = (
                scales[g][:].rearrange("p (e j) -> p e j", j=DH).unsqueeze(1).to_broadcast([P, TILES_PER_BANK, GROUP_HEADS, DH])
            )
            if g + LEAD >= GROUPS and quarter == 0:
                nc.scalar.copy(out=target, in_=h_tc[:].rearrange("p m (e j) -> p m e j", j=DH))
                nc.gpsimd.tensor_tensor(out=target, in0=target, in1=scale_rows, op=ALU.mult)
                return
            nc.vector.tensor_tensor(out=target, in0=h_tc[:].rearrange("p m (e j) -> p m e j", j=DH), in1=scale_rows, op=ALU.mult)

        def store(g):
            b, col0 = batch_and_columns(g)
            n, head0 = divmod(col0 // DH, H)
            nc.sync.dma_start(
                out=out[n, b, head0 : head0 + GROUP_HEADS].rearrange("e (q m) j -> q e (m j)", m=M_TILES),
                in_=staged[g][:].rearrange("p e m j -> p e (m j)"),
            )

        for g in range(-LEAD, GROUPS):
            if g + LEAD == GROUPS_PER_BATCH:
                quantise(1)
            if g >= 0:
                apply_gain(g)
            for quarter in range(QUARTERS):
                if 0 <= g + 1 < GROUPS:
                    if quarter == 0:
                        add_halves(g + 1)
                    elif quarter == 2:
                        inverse_root(g + 1)
                if g + LEAD < GROUPS:
                    statistics_pass(g + LEAD, quarter)
                if g >= 0:
                    output_bank(g, quarter)
            if 0 <= g + 1 < GROUPS:
                spread_over_partitions(g + 1)
            if g >= 0:
                store(g)
            else:
                leaky_relu(1, g + LEAD)
                if g == -1:
                    regroup_batch_1()
